import numpy as np
import ml_dtypes


def mxq(x, axis, fmt="e4m3"):
    dtype, down = {"e4m3": (ml_dtypes.float8_e4m3fn, 7), "e5m2": (ml_dtypes.float8_e5m2, 14)}[fmt]
    v = np.moveaxis(np.asarray(x, np.float32).astype(ml_dtypes.bfloat16).astype(np.float64), axis, -1)
    blocks = v.reshape(v.shape[:-1] + (-1, 32))
    amax = np.abs(blocks).max(-1, keepdims=True)
    byte = np.maximum(np.where(amax > 0, np.frexp(amax)[1] - 1 + 127, 0) - down, 1)
    scale = np.exp2(byte - 127.0)
    codes = (blocks / scale).astype(np.float32).astype(dtype).astype(np.float64)
    return np.moveaxis((codes * scale).reshape(v.shape), -1, axis)


WIDE = False


def mx_kscale(k):
    if not WIDE:
        return np.ones(k)
    levels = np.array([10, -10, 5, -5, 0])
    a = np.random.permutation(np.resize(levels, k // 512 * 4)).reshape(k // 512, 4)
    idx = np.arange(k)
    return np.exp2(a[idx // 512, idx % 128 // 32])


BF16 = ml_dtypes.bfloat16


def bf(x):
    return np.asarray(x, np.float32).astype(BF16)


def f64(x):
    return np.asarray(x).astype(np.float64)


E2M1 = np.array([0.0, 0.5, 1.0, 1.5, 2.0, 3.0, 4.0, 6.0, -0.0, -0.5, -1.0, -1.5, -2.0, -3.0, -4.0, -6.0])


def pack_weight(w, fmt):
    k, n = w.shape
    w = f64(bf(w)).reshape(k // 32, 32, n)
    amax = np.abs(w).max(1)
    if fmt == "e4m3":
        byte = np.frexp(amax)[1] - 1 + 127 - 7
    else:
        mant, ex = np.frexp(amax / 6.0)
        byte = np.where(mant > 0.5, ex, ex - 1) + 127
    byte = np.clip(np.where(amax > 0, byte, 1), 1, 254)
    scaled = (w * np.exp2(127.0 - byte)[:, None, :]).reshape(k, n).astype(np.float32)
    by_word = np.ascontiguousarray(scaled.reshape(k // 512, 128, 4, n).transpose(0, 1, 3, 2))
    if fmt == "e4m3":
        words = by_word.astype(ml_dtypes.float8_e4m3fn).view(np.uint8)
    else:
        c = by_word.astype(ml_dtypes.float4_e2m1fn).view(np.uint8) & 0xF
        words = c[..., 0::2] | (c[..., 1::2] << 4)
    return np.ascontiguousarray(words), np.ascontiguousarray(byte.astype(np.uint8).reshape(k // 512, 16, n))


def unpack_weight(words, scales, fmt):
    g, p, n, _ = words.shape
    if fmt == "e4m3":
        vals = np.ascontiguousarray(words).view(ml_dtypes.float8_e4m3fn).astype(np.float64)
    else:
        nib = np.empty((g, p, n, 4), np.uint8)
        nib[..., 0::2] = words & 0xF
        nib[..., 1::2] = words >> 4
        vals = E2M1[nib]
    vals = vals * np.repeat(np.exp2(scales.astype(np.float64) - 127.0), 8, axis=1)[..., None]
    return vals.transpose(0, 1, 3, 2).reshape(g * 512, n)

def pack4(w):
    words, scales = pack_weight(w, "e2m1")
    return words.reshape(words.shape[0], 128, -1), scales


def unpack4(words, scales):
    return unpack_weight(words.reshape(words.shape[0], 128, -1, 2), scales, "e2m1")


B, HEAD, NUM_EXPERTS, HEAD_DIM = 128, 1, 3, 2560
EPS = 1e-5
VAR0 = 3e-4


def setup_inputs():
    s = mx_kscale(HEAD_DIM)
    p = (HEAD, NUM_EXPERTS, HEAD_DIM)

    def draw_x():
        return bf((np.random.standard_normal((B, HEAD, HEAD_DIM)) * s).reshape(B, HEAD * HEAD_DIM))

    x1 = draw_x()
    x2 = draw_x()
    x3 = draw_x()
    W = np.random.standard_normal((HEAD, NUM_EXPERTS, HEAD_DIM, HEAD_DIM)) / np.sqrt(HEAD_DIM) / s
    cat = np.ascontiguousarray(np.swapaxes(W, -1, -2)).reshape(-1, HEAD_DIM)
    words, scales = pack4(cat)
    return {"x1": x1, "x2": x2, "x3": x3,
            "W_words": words, "W_scales": scales,
            "b": bf(np.random.standard_normal(p) * 0.3),
            "gamma": bf(np.sqrt(VAR0) * (1.0 + 0.1 * np.random.standard_normal(p))),
            "beta": bf(np.random.standard_normal(p) * 0.3),
            "running_mean": bf(np.random.standard_normal(p) * 0.3),
            "running_var": bf(VAR0 * np.random.uniform(0.5, 1.5, p))}


def reference(x1, x2, x3, W_words, W_scales, b, gamma, beta, running_mean, running_var):
    n = x1.shape[0]
    xs = np.stack([f64(x1).reshape(n, HEAD, HEAD_DIM),
                   f64(x2).reshape(n, HEAD, HEAD_DIM),
                   f64(x3).reshape(n, HEAD, HEAD_DIM)], axis=2)
    xq = mxq(xs, 3, "e4m3")
    wt = unpack4(W_words, W_scales).reshape(HEAD, NUM_EXPERTS, HEAD_DIM, HEAD_DIM)
    y = (xq.transpose(1, 2, 0, 3) @ wt).transpose(2, 0, 1, 3) + f64(b)
    y = y * (1.0 / (1.0 + np.exp(-1.702 * y)))
    y = (y - f64(running_mean)) * (1.0 / np.sqrt(f64(running_var) + EPS)) * f64(gamma) + f64(beta)
    return np.transpose(y, (0, 2, 1, 3)).reshape(n, NUM_EXPERTS * HEAD * HEAD_DIM)

@@ -1,0 +1,207 @@
+from contextlib import ExitStack
+
+import concourse.mybir as mybir
+from concourse.masks import make_identity
+
+F32 = mybir.dt.float32
+BF16 = mybir.dt.bfloat16
+I32 = mybir.dt.int32
+U8 = mybir.dt.uint8
+U32 = mybir.dt.uint32
+FP8X4 = mybir.dt.float8_e4m3fn_x4
+FP4X4 = mybir.dt.float4_e2m1fn_x4
+ACT = mybir.ActivationFunctionType
+ALU = mybir.AluOpType
+
+P = 128
+BATCH = 128
+EXPERTS = 3
+WIDTH = 2560
+K_PASS = 512
+PASSES = WIDTH // K_PASS
+F_TILE = 128
+TILES_PER_EXPERT = WIDTH // F_TILE
+TILES = EXPERTS * TILES_PER_EXPERT
+TILES_PER_BANK = 4
+BANKS = TILES // TILES_PER_BANK
+HALVES = 2
+TILES_PER_HALF = TILES_PER_EXPERT // HALVES
+HALF = WIDTH // HALVES
+BANKS_PER_ROUND = 2
+EPS = 1e-5
+
+FLOPS = 2 * BATCH * WIDTH * WIDTH * EXPERTS
+
+
+def tile_mom_w_e_kernel(
+    tc, x1, x2, x3, W_words, W_scales, b, gamma, beta, running_mean, running_var, out
+):
+    nc = tc.nc
+    xs = (x1, x2, x3)
+    vectors = (b, gamma, beta, running_mean, running_var)
+    with ExitStack() as stack:
+        keep = stack.enter_context(tc.tile_pool(name="keep", bufs=1))
+        stage = stack.enter_context(tc.tile_pool(name="stage", bufs=3))
+        late = stack.enter_context(tc.tile_pool(name="late", bufs=2 * BANKS_PER_ROUND))
+        psum_setup = stack.enter_context(tc.psum_pool(name="psum_setup", bufs=2))
+        psum_acc = stack.enter_context(tc.psum_pool(name="psum_acc", bufs=2 * BANKS_PER_ROUND))
+        psum_flip = stack.enter_context(tc.psum_pool(name="psum_flip", bufs=2))
+        stack.enter_context(tc.manual_schedule())
+
+        ident_f32 = keep.tile([P, P], F32)
+        make_identity(nc, ident_f32[:])
+        ident_bf16 = keep.tile([P, P], BF16)
+        make_identity(nc, ident_bf16[:])
+
+        rows = keep.tile([P, len(vectors), F_TILE], BF16)
+        nc.vector.memset(rows[:], 0.0)
+        w_planes = keep.tile([P, EXPERTS * PASSES, WIDTH], U8, align_bytes=64)
+        for e in range(EXPERTS):
+            nc.vector.memset(w_planes[:, PASSES * e : PASSES * (e + 1), :].bitcast(I32), 0)
+
+        for i, vector in enumerate(vectors):
+            nc.scalar.dma_start(
+                out=rows[0:TILES, i, :], in_=vector.rearrange("o e (j p) -> (o e j) p", p=F_TILE)
+            )
+        x_sb = []
+        for e in range(EXPERTS):
+            x_tile = keep.tile([BATCH, WIDTH], BF16, name="x_%d" % e)
+            nc.sync.dma_start(out=x_tile[:], in_=xs[e])
+            x_sb.append(x_tile)
+        words_i32 = W_words.bitcast(I32)
+        scales_i32 = W_scales.bitcast(I32)
+        w_words = []
+        for e in range(EXPERTS):
+            passes_e = slice(PASSES * e, PASSES * (e + 1))
+            for h in range(HALVES):
+                for first in (0, 1, 2, 3, 32, 33, 34, 35):
+                    q = 4 * (first // 32) + first % 32
+                    nc.sync.dma_start(
+                        out=w_planes[first:P:64, passes_e, HALF * h : HALF * (h + 1)].bitcast(I32),
+                        in_=scales_i32[
+                            passes_e, q:16:8, HALF // 4 * h : HALF // 4 * (h + 1)
+                        ].rearrange("g q n -> q g n"),
+                    )
+            halves = []
+            for h in range(HALVES):
+                w_tile = keep.tile([P, PASSES, 2 * HALF], U8, name="w_%d_%d" % (e, h), align_bytes=64)
+                nc.sync.dma_start(
+                    out=w_tile[:].bitcast(I32),
+                    in_=words_i32[passes_e, :, HALF // 2 * h : HALF // 2 * (h + 1)].rearrange(
+                        "g p c -> p g c"
+                    ),
+                )
+                halves.append(w_tile)
+            w_words.append(halves)
+
+        x_codes = keep.tile([P, EXPERTS * PASSES, BATCH], U32, align_bytes=64)
+        x_planes = keep.tile([P, EXPERTS * PASSES, BATCH], U8, align_bytes=64)
+        for e in range(EXPERTS):
+            x_pairs = x_sb[e][:].bitcast(F32)
+            for g in range(PASSES):
+                flipped_x = psum_setup.tile([P, 2, BATCH], F32, tag="setup")
+                for u in range(2):
+                    nc.tensor.transpose(
+                        flipped_x[:, u, :],
+                        x_pairs[:, K_PASS // 2 * g + u : K_PASS // 2 * (g + 1) : 2],
+                        ident_f32[:],
+                    )
+                grouped = stage.tile([P, 4 * BATCH], BF16, align_bytes=64)
+                nc.scalar.copy(
+                    out=grouped[:].bitcast(F32).rearrange("p (n u) -> p n u", u=2),
+                    in_=flipped_x[:].rearrange("p u n -> p n u"),
+                )
+                nc.vector.quantize_mx(
+                    out=x_codes[:, PASSES * e + g, :].bitcast(FP8X4),
+                    scales=x_planes[:, PASSES * e + g, :],
+                    in_=grouped[:],
+                )
+
+        flipped_rows = psum_setup.tile([P, len(vectors), P], BF16, tag="setup")
+        for i in range(len(vectors)):
+            nc.tensor.transpose(flipped_rows[:, i, :], rows[:, i, :], ident_bf16[:])
+        columns = keep.tile([P, len(vectors), TILES], F32)
+        nc.vector.tensor_copy(out=columns[:], in_=flipped_rows[:, :, 0:TILES])
+        bias_c = columns[:, 0, :]
+        gamma_c = columns[:, 1, :]
+        beta_c = columns[:, 2, :]
+        mean_c = columns[:, 3, :]
+        var_c = columns[:, 4, :]
+        var_eps = keep.tile([P, TILES], F32)
+        nc.vector.tensor_scalar_add(out=var_eps[:], in0=var_c, scalar1=EPS)
+        std = keep.tile([P, TILES], F32)
+        nc.scalar.sqrt(out=std[:], in_=var_eps[:])
+        rstd = keep.tile([P, TILES], F32)
+        nc.vector.reciprocal(out=rstd[:], in_=std[:])
+        gain = keep.tile([P, TILES], F32)
+        nc.vector.tensor_mul(out=gain[:], in0=gamma_c, in1=rstd[:])
+        mean_gain = keep.tile([P, TILES], F32)
+        nc.vector.tensor_mul(out=mean_gain[:], in0=mean_c, in1=gain[:])
+        shift = keep.tile([P, TILES], F32)
+        nc.vector.tensor_sub(out=shift[:], in0=beta_c, in1=mean_gain[:])
+
+        result = keep.tile([BATCH, EXPERTS * WIDTH], F32)
+        normed_of = {}
+
+        def multiply(bank):
+            acc = psum_acc.tile([P, TILES_PER_BANK, BATCH], F32)
+            for j in range(TILES_PER_BANK):
+                e, tile_e = divmod(TILES_PER_BANK * bank + j, TILES_PER_EXPERT)
+                h, tile_h = divmod(tile_e, TILES_PER_HALF)
+                for g in range(PASSES):
+                    nc.tensor.matmul_mx(
+                        out=acc[:, j, :],
+                        lhsT=w_words[e][h][:, g, 2 * F_TILE * tile_h : 2 * F_TILE * (tile_h + 1)].bitcast(FP4X4),
+                        lhsT_scale=w_planes[:, PASSES * e + g, F_TILE * tile_e : F_TILE * (tile_e + 1)],
+                        rhs=x_codes[:, PASSES * e + g, :].bitcast(FP8X4),
+                        rhs_scale=x_planes[:, PASSES * e + g, :],
+                        start=(g == 0),
+                        stop=(g == PASSES - 1),
+                    )
+            gelu = stage.tile([P, TILES_PER_BANK, BATCH], F32)
+            normed = late.tile([P, TILES_PER_BANK, BATCH], F32)
+            for j in reversed(range(TILES_PER_BANK)):
+                column = TILES_PER_BANK * bank + j
+                nc.scalar.activation(
+                    out=gelu[:, j, :],
+                    in_=acc[:, j, :],
+                    func=ACT.Gelu_apprx_sigmoid,
+                    bias=bias_c[:, column : column + 1],
+                    scale=1.0,
+                )
+                nc.vector.tensor_scalar(
+                    out=normed[:, j, :],
+                    in0=gelu[:, j, :],
+                    scalar1=gain[:, column : column + 1],
+                    scalar2=shift[:, column : column + 1],
+                    op0=ALU.mult,
+                    op1=ALU.add,
+                )
+            normed_of[bank] = normed
+
+        def finish(banks):
+            for bank in banks:
+                flipped = psum_flip.tile([BATCH, TILES_PER_BANK, F_TILE], F32)
+                for j in range(TILES_PER_BANK):
+                    nc.tensor.transpose(flipped[:, j, :], normed_of[bank][:, j, :], ident_f32[:])
+                columns_of_bank = slice(TILES_PER_BANK * F_TILE * bank, TILES_PER_BANK * F_TILE * (bank + 1))
+                if bank % 2 == 0:
+                    nc.vector.tensor_copy(
+                        out=result[:, columns_of_bank], in_=flipped[:].rearrange("n j f -> n (j f)")
+                    )
+                else:
+                    nc.scalar.copy(
+                        out=result[:, columns_of_bank], in_=flipped[:].rearrange("n j f -> n (j f)")
+                    )
+            columns_of_round = slice(TILES_PER_BANK * F_TILE * banks[0], TILES_PER_BANK * F_TILE * (banks[-1] + 1))
+            nc.sync.dma_start(out=out[:, columns_of_round], in_=result[:, columns_of_round])
+
+        rounds = [
+            list(range(first, min(first + BANKS_PER_ROUND, BANKS))) for first in range(0, BANKS, BANKS_PER_ROUND)
+        ]
+        for r, banks in enumerate(rounds):
+            for bank in banks:
+                multiply(bank)
+            if r > 0:
+                finish(rounds[r - 1])
+        finish(rounds[-1])

@@ -73,14 +73,12 @@ def tile_mom_w_e_kernel(
         w_words = []
         for e in range(EXPERTS):
             passes_e = slice(PASSES * e, PASSES * (e + 1))
-            for h in range(HALVES):
+            for some_passes in (slice(PASSES * e, PASSES * e + 3), slice(PASSES * e + 3, PASSES * (e + 1))):
                 for first in (0, 1, 2, 3, 32, 33, 34, 35):
                     q = 4 * (first // 32) + first % 32
                     nc.sync.dma_start(
-                        out=w_planes[first:P:64, passes_e, HALF * h : HALF * (h + 1)].bitcast(I32),
-                        in_=scales_i32[
-                            passes_e, q:16:8, HALF // 4 * h : HALF // 4 * (h + 1)
-                        ].rearrange("g q n -> q g n"),
+                        out=w_planes[first:P:64, some_passes, :].bitcast(I32),
+                        in_=scales_i32[some_passes, q:16:8, :].rearrange("g q n -> q g n"),
                     )
             halves = []
             for h in range(HALVES):

@@ -24,10 +24,9 @@ TILES_PER_EXPERT = WIDTH // F_TILE
 TILES = EXPERTS * TILES_PER_EXPERT
 TILES_PER_BANK = 4
 BANKS = TILES // TILES_PER_BANK
-HALVES = 2
-TILES_PER_HALF = TILES_PER_EXPERT // HALVES
-HALF = WIDTH // HALVES
-BANKS_PER_ROUND = 2
+CHUNKS = ((10, 10), (10, 10), (10, 10))
+PASSES_PER_UNIT = 2
+GROUPS_PER_ROUND = 2
 EPS = 1e-5
 
 FLOPS = 2 * BATCH * WIDTH * WIDTH * EXPERTS
@@ -42,37 +41,54 @@ def tile_mom_w_e_kernel(
     with ExitStack() as stack:
         keep = stack.enter_context(tc.tile_pool(name="keep", bufs=1))
         stage = stack.enter_context(tc.tile_pool(name="stage", bufs=3))
-        late = stack.enter_context(tc.tile_pool(name="late", bufs=2 * BANKS_PER_ROUND))
-        psum_setup = stack.enter_context(tc.psum_pool(name="psum_setup", bufs=2))
-        psum_acc = stack.enter_context(tc.psum_pool(name="psum_acc", bufs=2 * BANKS_PER_ROUND))
-        psum_flip = stack.enter_context(tc.psum_pool(name="psum_flip", bufs=2))
+        late = stack.enter_context(tc.tile_pool(name="late", bufs=2 * GROUPS_PER_ROUND))
+        psum_acc = stack.enter_context(tc.psum_pool(name="psum_acc", bufs=2 * GROUPS_PER_ROUND))
+        psum_turn = stack.enter_context(tc.psum_pool(name="psum_turn", bufs=4))
         stack.enter_context(tc.manual_schedule())
 
         ident_f32 = keep.tile([P, P], F32)
         make_identity(nc, ident_f32[:])
-        ident_bf16 = keep.tile([P, P], BF16)
-        make_identity(nc, ident_bf16[:])
 
         rows = keep.tile([P, len(vectors), F_TILE], BF16)
         nc.vector.memset(rows[:], 0.0)
+        ident_bf16 = keep.tile([P, P], BF16)
+        make_identity(nc, ident_bf16[:])
         w_planes = keep.tile([P, EXPERTS * PASSES, WIDTH], U8, align_bytes=64)
-        for e in range(EXPERTS):
+
+        def zero_planes(e):
             nc.vector.memset(w_planes[:, PASSES * e : PASSES * (e + 1), :].bitcast(I32), 0)
 
         for i, vector in enumerate(vectors):
             nc.scalar.dma_start(
                 out=rows[0:TILES, i, :], in_=vector.rearrange("o e (j p) -> (o e j) p", p=F_TILE)
             )
-        x_sb = []
-        for e in range(EXPERTS):
-            x_tile = keep.tile([BATCH, WIDTH], BF16, name="x_%d" % e)
-            nc.sync.dma_start(out=x_tile[:], in_=xs[e])
-            x_sb.append(x_tile)
+        one = keep.tile([P, 1], F32)
+        nc.vector.memset(one[:], 1.0)
+        warm = keep.tile([P, 2], F32)
+        nc.scalar.sqrt(out=warm[:, 0:1], in_=one[:])
+        x_sb = {}
         words_i32 = W_words.bitcast(I32)
         scales_i32 = W_scales.bitcast(I32)
-        w_words = []
-        for e in range(EXPERTS):
+        w_words = {}
+
+        def load_x(e):
+            x_tile = keep.tile([BATCH, WIDTH], BF16, name="x_%d" % e)
+            nc.sync.dma_start(out=x_tile[:], in_=xs[e])
+            x_sb[e] = x_tile
+
+        def load_chunk(e, first_tile, tiles):
             passes_e = slice(PASSES * e, PASSES * (e + 1))
+            first_f = F_TILE * first_tile
+            features = F_TILE * tiles
+            w_tile = keep.tile([P, PASSES, 2 * features], U8, name="w_%d_%d" % (e, first_tile), align_bytes=64)
+            nc.sync.dma_start(
+                out=w_tile[:].bitcast(I32),
+                in_=words_i32[passes_e, :, first_f // 2 : (first_f + features) // 2].rearrange("g p c -> p g c"),
+            )
+            for t in range(tiles):
+                w_words[(e, first_tile + t)] = (w_tile, t)
+
+        def load_expert(e):
             for some_passes in (slice(PASSES * e, PASSES * e + 3), slice(PASSES * e + 3, PASSES * (e + 1))):
                 for first in (0, 1, 2, 3, 32, 33, 34, 35):
                     q = 4 * (first // 32) + first % 32
@@ -80,126 +96,163 @@ def tile_mom_w_e_kernel(
                         out=w_planes[first:P:64, some_passes, :].bitcast(I32),
                         in_=scales_i32[some_passes, q:16:8, :].rearrange("g q n -> q g n"),
                     )
-            halves = []
-            for h in range(HALVES):
-                w_tile = keep.tile([P, PASSES, 2 * HALF], U8, name="w_%d_%d" % (e, h), align_bytes=64)
-                nc.sync.dma_start(
-                    out=w_tile[:].bitcast(I32),
-                    in_=words_i32[passes_e, :, HALF // 2 * h : HALF // 2 * (h + 1)].rearrange(
-                        "g p c -> p g c"
-                    ),
-                )
-                halves.append(w_tile)
-            w_words.append(halves)
+            first_tile = 0
+            for tiles in CHUNKS[e]:
+                load_chunk(e, first_tile, tiles)
+                first_tile += tiles
+
+        zero_planes(0)
+        for e in range(EXPERTS):
+            load_x(e)
+        load_expert(0)
 
         x_codes = keep.tile([P, EXPERTS * PASSES, BATCH], U32, align_bytes=64)
         x_planes = keep.tile([P, EXPERTS * PASSES, BATCH], U8, align_bytes=64)
-        for e in range(EXPERTS):
-            x_pairs = x_sb[e][:].bitcast(F32)
-            for g in range(PASSES):
-                flipped_x = psum_setup.tile([P, 2, BATCH], F32, tag="setup")
+
+        grouped_of = {}
+
+        def turn_x(unit, first, count):
+            turned = psum_turn.tile([P, PASSES_PER_UNIT, 2, BATCH], F32, tag="turn")
+            for a in range(count):
+                e, g = divmod(first + a, PASSES)
+                x_pairs = x_sb[e][:].bitcast(F32)
                 for u in range(2):
                     nc.tensor.transpose(
-                        flipped_x[:, u, :],
+                        turned[:, a, u, :],
                         x_pairs[:, K_PASS // 2 * g + u : K_PASS // 2 * (g + 1) : 2],
                         ident_f32[:],
                     )
-                grouped = stage.tile([P, 4 * BATCH], BF16, align_bytes=64)
-                nc.scalar.copy(
-                    out=grouped[:].bitcast(F32).rearrange("p (n u) -> p n u", u=2),
-                    in_=flipped_x[:].rearrange("p u n -> p n u"),
-                )
-                nc.vector.quantize_mx(
-                    out=x_codes[:, PASSES * e + g, :].bitcast(FP8X4),
-                    scales=x_planes[:, PASSES * e + g, :],
-                    in_=grouped[:],
-                )
+            grouped = stage.tile([P, PASSES_PER_UNIT, 4 * BATCH], BF16, align_bytes=64)
+            copy_out = grouped[:, 0:count, :].bitcast(F32).rearrange("p a (n u) -> p a n u", u=2)
+            copy_in = turned[:, 0:count, :, :].rearrange("p a u n -> p a n u")
+            if unit % 2 == 0:
+                nc.scalar.copy(out=copy_out, in_=copy_in)
+            else:
+                nc.vector.tensor_copy(out=copy_out, in_=copy_in)
+            grouped_of[unit] = grouped
 
-        flipped_rows = psum_setup.tile([P, len(vectors), P], BF16, tag="setup")
-        for i in range(len(vectors)):
-            nc.tensor.transpose(flipped_rows[:, i, :], rows[:, i, :], ident_bf16[:])
+        def quantise_x(unit, first, count):
+            nc.vector.quantize_mx(
+                out=x_codes[:, first : first + count, :].rearrange("p a n -> p (a n)").bitcast(FP8X4),
+                scales=x_planes[:, first : first + count, :].rearrange("p a n -> p (a n)"),
+                in_=grouped_of[unit][:, 0:count, :].rearrange("p a c -> p (a c)"),
+            )
+
+        units = [
+            (first, min(PASSES_PER_UNIT, EXPERTS * PASSES - first))
+            for first in range(0, EXPERTS * PASSES, PASSES_PER_UNIT)
+        ]
+        for unit, (first, count) in enumerate(units):
+            turn_x(unit, first, count)
+            if unit > 0:
+                quantise_x(unit - 1, units[unit - 1][0], units[unit - 1][1])
+        quantise_x(len(units) - 1, units[-1][0], units[-1][1])
+        for e in range(1, EXPERTS):
+            zero_planes(e)
+            load_expert(e)
+
         columns = keep.tile([P, len(vectors), TILES], F32)
-        nc.vector.tensor_copy(out=columns[:], in_=flipped_rows[:, :, 0:TILES])
-        bias_c = columns[:, 0, :]
-        gamma_c = columns[:, 1, :]
-        beta_c = columns[:, 2, :]
-        mean_c = columns[:, 3, :]
-        var_c = columns[:, 4, :]
-        var_eps = keep.tile([P, TILES], F32)
-        nc.vector.tensor_scalar_add(out=var_eps[:], in0=var_c, scalar1=EPS)
-        std = keep.tile([P, TILES], F32)
-        nc.scalar.sqrt(out=std[:], in_=var_eps[:])
-        rstd = keep.tile([P, TILES], F32)
-        nc.vector.reciprocal(out=rstd[:], in_=std[:])
         gain = keep.tile([P, TILES], F32)
-        nc.vector.tensor_mul(out=gain[:], in0=gamma_c, in1=rstd[:])
-        mean_gain = keep.tile([P, TILES], F32)
-        nc.vector.tensor_mul(out=mean_gain[:], in0=mean_c, in1=gain[:])
         shift = keep.tile([P, TILES], F32)
-        nc.vector.tensor_sub(out=shift[:], in0=beta_c, in1=mean_gain[:])
+
+        def prepare_vectors():
+            flipped_rows = psum_turn.tile([P, len(vectors), P], BF16, tag="turn")
+            for i in range(len(vectors)):
+                nc.tensor.transpose(flipped_rows[:, i, :], rows[:, i, :], ident_bf16[:])
+            nc.vector.tensor_copy(out=columns[:], in_=flipped_rows[:, :, 0:TILES])
+            gamma_c = columns[:, 1, :]
+            beta_c = columns[:, 2, :]
+            mean_c = columns[:, 3, :]
+            var_c = columns[:, 4, :]
+            var_eps = keep.tile([P, TILES], F32)
+            nc.vector.tensor_scalar_add(out=var_eps[:], in0=var_c, scalar1=EPS)
+            std = keep.tile([P, TILES], F32)
+            nc.scalar.sqrt(out=std[:], in_=var_eps[:])
+            nc.scalar.activation(out=warm[:, 1:2], in_=one[:], func=ACT.Gelu_apprx_sigmoid)
+            rstd = keep.tile([P, TILES], F32)
+            nc.vector.reciprocal(out=rstd[:], in_=std[:])
+            nc.vector.tensor_mul(out=gain[:], in0=gamma_c, in1=rstd[:])
+            mean_gain = keep.tile([P, TILES], F32)
+            nc.vector.tensor_mul(out=mean_gain[:], in0=mean_c, in1=gain[:])
+            nc.vector.tensor_sub(out=shift[:], in0=beta_c, in1=mean_gain[:])
 
         result = keep.tile([BATCH, EXPERTS * WIDTH], F32)
+        acc_of = {}
         normed_of = {}
 
-        def multiply(bank):
+        def multiply(group):
             acc = psum_acc.tile([P, TILES_PER_BANK, BATCH], F32)
-            for j in range(TILES_PER_BANK):
-                e, tile_e = divmod(TILES_PER_BANK * bank + j, TILES_PER_EXPERT)
-                h, tile_h = divmod(tile_e, TILES_PER_HALF)
+            for j, tile in enumerate(groups[group]):
+                e, tile_e = divmod(tile, TILES_PER_EXPERT)
+                w_tile, t = w_words[(e, tile_e)]
                 for g in range(PASSES):
                     nc.tensor.matmul_mx(
                         out=acc[:, j, :],
-                        lhsT=w_words[e][h][:, g, 2 * F_TILE * tile_h : 2 * F_TILE * (tile_h + 1)].bitcast(FP4X4),
+                        lhsT=w_tile[:, g, 2 * F_TILE * t : 2 * F_TILE * (t + 1)].bitcast(FP4X4),
                         lhsT_scale=w_planes[:, PASSES * e + g, F_TILE * tile_e : F_TILE * (tile_e + 1)],
                         rhs=x_codes[:, PASSES * e + g, :].bitcast(FP8X4),
                         rhs_scale=x_planes[:, PASSES * e + g, :],
                         start=(g == 0),
                         stop=(g == PASSES - 1),
                     )
+            acc_of[group] = acc
+
+        def activate(group):
+            acc = acc_of[group]
             gelu = stage.tile([P, TILES_PER_BANK, BATCH], F32)
             normed = late.tile([P, TILES_PER_BANK, BATCH], F32)
-            for j in reversed(range(TILES_PER_BANK)):
-                column = TILES_PER_BANK * bank + j
+            for j, tile in reversed(list(enumerate(groups[group]))):
                 nc.scalar.activation(
                     out=gelu[:, j, :],
                     in_=acc[:, j, :],
                     func=ACT.Gelu_apprx_sigmoid,
-                    bias=bias_c[:, column : column + 1],
+                    bias=columns[:, 0, tile : tile + 1],
                     scale=1.0,
                 )
                 nc.vector.tensor_scalar(
                     out=normed[:, j, :],
                     in0=gelu[:, j, :],
-                    scalar1=gain[:, column : column + 1],
-                    scalar2=shift[:, column : column + 1],
+                    scalar1=gain[:, tile : tile + 1],
+                    scalar2=shift[:, tile : tile + 1],
                     op0=ALU.mult,
                     op1=ALU.add,
                 )
-            normed_of[bank] = normed
+            normed_of[group] = normed
 
-        def finish(banks):
-            for bank in banks:
-                flipped = psum_flip.tile([BATCH, TILES_PER_BANK, F_TILE], F32)
-                for j in range(TILES_PER_BANK):
-                    nc.tensor.transpose(flipped[:, j, :], normed_of[bank][:, j, :], ident_f32[:])
-                columns_of_bank = slice(TILES_PER_BANK * F_TILE * bank, TILES_PER_BANK * F_TILE * (bank + 1))
-                if bank % 2 == 0:
+        def finish(round_groups):
+            for group in round_groups:
+                tiles = groups[group]
+                flipped = psum_turn.tile([BATCH, TILES_PER_BANK, F_TILE], F32, tag="turn")
+                for j in range(len(tiles)):
+                    nc.tensor.transpose(flipped[:, j, :], normed_of[group][:, j, :], ident_f32[:])
+                columns_of_group = slice(F_TILE * tiles[0], F_TILE * (tiles[-1] + 1))
+                if group % 2 == 0:
                     nc.vector.tensor_copy(
-                        out=result[:, columns_of_bank], in_=flipped[:].rearrange("n j f -> n (j f)")
+                        out=result[:, columns_of_group],
+                        in_=flipped[:, 0 : len(tiles), :].rearrange("n j f -> n (j f)"),
                     )
                 else:
                     nc.scalar.copy(
-                        out=result[:, columns_of_bank], in_=flipped[:].rearrange("n j f -> n (j f)")
+                        out=result[:, columns_of_group],
+                        in_=flipped[:, 0 : len(tiles), :].rearrange("n j f -> n (j f)"),
                     )
-            columns_of_round = slice(TILES_PER_BANK * F_TILE * banks[0], TILES_PER_BANK * F_TILE * (banks[-1] + 1))
+            columns_of_round = slice(
+                F_TILE * groups[round_groups[0]][0], F_TILE * (groups[round_groups[-1]][-1] + 1)
+            )
             nc.sync.dma_start(out=out[:, columns_of_round], in_=result[:, columns_of_round])
 
+        groups = [list(range(first, first + TILES_PER_BANK)) for first in range(0, TILES - TILES_PER_BANK, TILES_PER_BANK)]
+        groups.append([TILES - 4, TILES - 3])
+        groups.append([TILES - 2, TILES - 1])
         rounds = [
-            list(range(first, min(first + BANKS_PER_ROUND, BANKS))) for first in range(0, BANKS, BANKS_PER_ROUND)
+            list(range(first, first + GROUPS_PER_ROUND)) for first in range(0, len(groups), GROUPS_PER_ROUND)
         ]
-        for r, banks in enumerate(rounds):
-            for bank in banks:
-                multiply(bank)
+        prepare_vectors()
+        for r, round_groups in enumerate(rounds):
+            for group in round_groups:
+                multiply(group)
+            for group in round_groups:
+                activate(group)
             if r > 0:
                 finish(rounds[r - 1])
         finish(rounds[-1])

from contextlib import ExitStack

import concourse.mybir as mybir
from concourse.masks import make_identity

F32 = mybir.dt.float32
BF16 = mybir.dt.bfloat16
I32 = mybir.dt.int32
U8 = mybir.dt.uint8
U32 = mybir.dt.uint32
FP8X4 = mybir.dt.float8_e4m3fn_x4
FP4X4 = mybir.dt.float4_e2m1fn_x4
ACT = mybir.ActivationFunctionType
ALU = mybir.AluOpType

P = 128
BATCH = 128
EXPERTS = 3
WIDTH = 2560
K_PASS = 512
PASSES = WIDTH // K_PASS
F_TILE = 128
TILES_PER_EXPERT = WIDTH // F_TILE
TILES = EXPERTS * TILES_PER_EXPERT
TILES_PER_BANK = 4
BANKS = TILES // TILES_PER_BANK
CHUNKS = ((10, 10), (10, 10), (10, 10))
PASSES_PER_UNIT = 2
GROUPS_PER_ROUND = 2
EPS = 1e-5

FLOPS = 2 * BATCH * WIDTH * WIDTH * EXPERTS


def tile_mom_w_e_kernel(
    tc, x1, x2, x3, W_words, W_scales, b, gamma, beta, running_mean, running_var, out
):
    nc = tc.nc
    xs = (x1, x2, x3)
    vectors = (b, gamma, beta, running_mean, running_var)
    with ExitStack() as stack:
        keep = stack.enter_context(tc.tile_pool(name="keep", bufs=1))
        stage = stack.enter_context(tc.tile_pool(name="stage", bufs=3))
        late = stack.enter_context(tc.tile_pool(name="late", bufs=2 * GROUPS_PER_ROUND))
        psum_acc = stack.enter_context(tc.psum_pool(name="psum_acc", bufs=2 * GROUPS_PER_ROUND))
        psum_turn = stack.enter_context(tc.psum_pool(name="psum_turn", bufs=4))
        stack.enter_context(tc.manual_schedule())

        ident_f32 = keep.tile([P, P], F32)
        make_identity(nc, ident_f32[:])

        rows = keep.tile([P, len(vectors), F_TILE], BF16)
        nc.vector.memset(rows[:], 0.0)
        ident_bf16 = keep.tile([P, P], BF16)
        make_identity(nc, ident_bf16[:])
        w_planes = keep.tile([P, EXPERTS * PASSES, WIDTH], U8, align_bytes=64)

        def zero_planes(e):
            nc.vector.memset(w_planes[:, PASSES * e : PASSES * (e + 1), :].bitcast(I32), 0)

        for i, vector in enumerate(vectors):
            nc.scalar.dma_start(
                out=rows[0:TILES, i, :], in_=vector.rearrange("o e (j p) -> (o e j) p", p=F_TILE)
            )
        one = keep.tile([P, 1], F32)
        nc.vector.memset(one[:], 1.0)
        warm = keep.tile([P, 2], F32)
        nc.scalar.sqrt(out=warm[:, 0:1], in_=one[:])
        x_sb = {}
        words_i32 = W_words.bitcast(I32)
        scales_i32 = W_scales.bitcast(I32)
        w_words = {}

        def load_x(e):
            x_tile = keep.tile([BATCH, WIDTH], BF16, name="x_%d" % e)
            nc.sync.dma_start(out=x_tile[:], in_=xs[e])
            x_sb[e] = x_tile

        def load_chunk(e, first_tile, tiles):
            passes_e = slice(PASSES * e, PASSES * (e + 1))
            first_f = F_TILE * first_tile
            features = F_TILE * tiles
            w_tile = keep.tile([P, PASSES, 2 * features], U8, name="w_%d_%d" % (e, first_tile), align_bytes=64)
            nc.sync.dma_start(
                out=w_tile[:].bitcast(I32),
                in_=words_i32[passes_e, :, first_f // 2 : (first_f + features) // 2].rearrange("g p c -> p g c"),
            )
            for t in range(tiles):
                w_words[(e, first_tile + t)] = (w_tile, t)

        def load_expert(e):
            for some_passes in (slice(PASSES * e, PASSES * e + 3), slice(PASSES * e + 3, PASSES * (e + 1))):
                for first in (0, 1, 2, 3, 32, 33, 34, 35):
                    q = 4 * (first // 32) + first % 32
                    nc.sync.dma_start(
                        out=w_planes[first:P:64, some_passes, :].bitcast(I32),
                        in_=scales_i32[some_passes, q:16:8, :].rearrange("g q n -> q g n"),
                    )
            first_tile = 0
            for tiles in CHUNKS[e]:
                load_chunk(e, first_tile, tiles)
                first_tile += tiles

        zero_planes(0)
        for e in range(EXPERTS):
            load_x(e)
        load_expert(0)

        x_codes = keep.tile([P, EXPERTS * PASSES, BATCH], U32, align_bytes=64)
        x_planes = keep.tile([P, EXPERTS * PASSES, BATCH], U8, align_bytes=64)

        grouped_of = {}

        def turn_x(unit, first, count):
            turned = psum_turn.tile([P, PASSES_PER_UNIT, 2, BATCH], F32, tag="turn")
            for a in range(count):
                e, g = divmod(first + a, PASSES)
                x_pairs = x_sb[e][:].bitcast(F32)
                for u in range(2):
                    nc.tensor.transpose(
                        turned[:, a, u, :],
                        x_pairs[:, K_PASS // 2 * g + u : K_PASS // 2 * (g + 1) : 2],
                        ident_f32[:],
                    )
            grouped = stage.tile([P, PASSES_PER_UNIT, 4 * BATCH], BF16, align_bytes=64)
            copy_out = grouped[:, 0:count, :].bitcast(F32).rearrange("p a (n u) -> p a n u", u=2)
            copy_in = turned[:, 0:count, :, :].rearrange("p a u n -> p a n u")
            if unit % 2 == 0:
                nc.scalar.copy(out=copy_out, in_=copy_in)
            else:
                nc.vector.tensor_copy(out=copy_out, in_=copy_in)
            grouped_of[unit] = grouped

        def quantise_x(unit, first, count):
            nc.vector.quantize_mx(
                out=x_codes[:, first : first + count, :].rearrange("p a n -> p (a n)").bitcast(FP8X4),
                scales=x_planes[:, first : first + count, :].rearrange("p a n -> p (a n)"),
                in_=grouped_of[unit][:, 0:count, :].rearrange("p a c -> p (a c)"),
            )

        units = [
            (first, min(PASSES_PER_UNIT, EXPERTS * PASSES - first))
            for first in range(0, EXPERTS * PASSES, PASSES_PER_UNIT)
        ]
        for unit, (first, count) in enumerate(units):
            turn_x(unit, first, count)
            if unit > 0:
                quantise_x(unit - 1, units[unit - 1][0], units[unit - 1][1])
        quantise_x(len(units) - 1, units[-1][0], units[-1][1])
        for e in range(1, EXPERTS):
            zero_planes(e)
            load_expert(e)

        columns = keep.tile([P, len(vectors), TILES], F32)
        gain = keep.tile([P, TILES], F32)
        shift = keep.tile([P, TILES], F32)

        def prepare_vectors():
            flipped_rows = psum_turn.tile([P, len(vectors), P], BF16, tag="turn")
            for i in range(len(vectors)):
                nc.tensor.transpose(flipped_rows[:, i, :], rows[:, i, :], ident_bf16[:])
            nc.vector.tensor_copy(out=columns[:], in_=flipped_rows[:, :, 0:TILES])
            gamma_c = columns[:, 1, :]
            beta_c = columns[:, 2, :]
            mean_c = columns[:, 3, :]
            var_c = columns[:, 4, :]
            var_eps = keep.tile([P, TILES], F32)
            nc.vector.tensor_scalar_add(out=var_eps[:], in0=var_c, scalar1=EPS)
            std = keep.tile([P, TILES], F32)
            nc.scalar.sqrt(out=std[:], in_=var_eps[:])
            nc.scalar.activation(out=warm[:, 1:2], in_=one[:], func=ACT.Gelu_apprx_sigmoid)
            rstd = keep.tile([P, TILES], F32)
            nc.vector.reciprocal(out=rstd[:], in_=std[:])
            nc.vector.tensor_mul(out=gain[:], in0=gamma_c, in1=rstd[:])
            mean_gain = keep.tile([P, TILES], F32)
            nc.vector.tensor_mul(out=mean_gain[:], in0=mean_c, in1=gain[:])
            nc.vector.tensor_sub(out=shift[:], in0=beta_c, in1=mean_gain[:])

        result = keep.tile([BATCH, EXPERTS * WIDTH], F32)
        acc_of = {}
        normed_of = {}

        def multiply(group):
            acc = psum_acc.tile([P, TILES_PER_BANK, BATCH], F32)
            for j, tile in enumerate(groups[group]):
                e, tile_e = divmod(tile, TILES_PER_EXPERT)
                w_tile, t = w_words[(e, tile_e)]
                for g in range(PASSES):
                    nc.tensor.matmul_mx(
                        out=acc[:, j, :],
                        lhsT=w_tile[:, g, 2 * F_TILE * t : 2 * F_TILE * (t + 1)].bitcast(FP4X4),
                        lhsT_scale=w_planes[:, PASSES * e + g, F_TILE * tile_e : F_TILE * (tile_e + 1)],
                        rhs=x_codes[:, PASSES * e + g, :].bitcast(FP8X4),
                        rhs_scale=x_planes[:, PASSES * e + g, :],
                        start=(g == 0),
                        stop=(g == PASSES - 1),
                    )
            acc_of[group] = acc

        def activate(group):
            acc = acc_of[group]
            gelu = stage.tile([P, TILES_PER_BANK, BATCH], F32)
            normed = late.tile([P, TILES_PER_BANK, BATCH], F32)
            for j, tile in reversed(list(enumerate(groups[group]))):
                nc.scalar.activation(
                    out=gelu[:, j, :],
                    in_=acc[:, j, :],
                    func=ACT.Gelu_apprx_sigmoid,
                    bias=columns[:, 0, tile : tile + 1],
                    scale=1.0,
                )
                nc.vector.tensor_scalar(
                    out=normed[:, j, :],
                    in0=gelu[:, j, :],
                    scalar1=gain[:, tile : tile + 1],
                    scalar2=shift[:, tile : tile + 1],
                    op0=ALU.mult,
                    op1=ALU.add,
                )
            normed_of[group] = normed

        def finish(round_groups):
            for group in round_groups:
                tiles = groups[group]
                flipped = psum_turn.tile([BATCH, TILES_PER_BANK, F_TILE], F32, tag="turn")
                for j in range(len(tiles)):
                    nc.tensor.transpose(flipped[:, j, :], normed_of[group][:, j, :], ident_f32[:])
                columns_of_group = slice(F_TILE * tiles[0], F_TILE * (tiles[-1] + 1))
                if group % 2 == 0:
                    nc.vector.tensor_copy(
                        out=result[:, columns_of_group],
                        in_=flipped[:, 0 : len(tiles), :].rearrange("n j f -> n (j f)"),
                    )
                else:
                    nc.scalar.copy(
                        out=result[:, columns_of_group],
                        in_=flipped[:, 0 : len(tiles), :].rearrange("n j f -> n (j f)"),
                    )
            columns_of_round = slice(
                F_TILE * groups[round_groups[0]][0], F_TILE * (groups[round_groups[-1]][-1] + 1)
            )
            nc.sync.dma_start(out=out[:, columns_of_round], in_=result[:, columns_of_round])

        groups = [list(range(first, first + TILES_PER_BANK)) for first in range(0, TILES - TILES_PER_BANK, TILES_PER_BANK)]
        groups.append([TILES - 4, TILES - 3])
        groups.append([TILES - 2, TILES - 1])
        rounds = [
            list(range(first, first + GROUPS_PER_ROUND)) for first in range(0, len(groups), GROUPS_PER_ROUND)
        ]
        prepare_vectors()
        for r, round_groups in enumerate(rounds):
            for group in round_groups:
                multiply(group)
            for group in round_groups:
                activate(group)
            if r > 0:
                finish(rounds[r - 1])
        finish(rounds[-1])
